import numpy as np
import ml_dtypes


def mxq(x, axis, fmt="e4m3"):
    dtype, down = {"e4m3": (ml_dtypes.float8_e4m3fn, 7), "e5m2": (ml_dtypes.float8_e5m2, 14)}[fmt]
    v = np.moveaxis(np.asarray(x, np.float32).astype(ml_dtypes.bfloat16).astype(np.float64), axis, -1)
    blocks = v.reshape(v.shape[:-1] + (-1, 32))
    amax = np.abs(blocks).max(-1, keepdims=True)
    byte = np.maximum(np.where(amax > 0, np.frexp(amax)[1] - 1 + 127, 0) - down, 1)
    scale = np.exp2(byte - 127.0)
    codes = (blocks / scale).astype(np.float32).astype(dtype).astype(np.float64)
    return np.moveaxis((codes * scale).reshape(v.shape), -1, axis)


WIDE = False


def mx_kscale(k):
    if not WIDE:
        return np.ones(k)
    levels = np.array([10, -10, 5, -5, 0])
    if k % 512:
        return np.exp2(np.random.permutation(np.resize(levels, k // 32))).repeat(32)
    a = np.empty((k // 512, 16))
    for p in range(k // 512):
        a[p, :8] = np.random.permutation(np.resize(levels, 8))
        for g in range(8):
            far = levels[np.abs(levels - a[p, g]) >= 10]
            a[p, g + 8] = far[np.random.randint(len(far))]
    return np.exp2(a.ravel()).repeat(32)


BF16 = ml_dtypes.bfloat16


def bf(x):
    return np.asarray(x, np.float32).astype(BF16)


def f64(x):
    return np.asarray(x).astype(np.float64)


B, NC, APC, D = 4096, 1, 512, 512
H = 2 * D
LN_EPS = 1e-5


def setup_inputs():
    s = mx_kscale(APC)
    t = np.exp2(np.round(np.log2(mx_kscale(H)) / 2))
    return {"tri": bf(np.random.standard_normal((B, APC * NC)) * np.repeat(s, NC)),
            "W1": bf(np.random.standard_normal((NC, APC, H)) / np.sqrt(APC) / s[None, :, None] * t),
            "b1": bf(np.random.standard_normal((NC, H)) * 0.1 * t),
            "W2": bf(np.random.standard_normal((NC, H, D)) / np.sqrt(H) / (t * t)[None, :, None]),
            "b2": bf(np.random.standard_normal((NC, D)) * 0.1),
            "gamma": bf(1.0 + 0.1 * np.random.standard_normal((NC, D))),
            "beta": bf(np.random.standard_normal((NC, D)) * 0.1)}


def reference(tri, W1, b1, W2, b2, gamma, beta):
    tri, W1, b1, W2, b2, gamma, beta = f64(tri), f64(W1), f64(b1), f64(W2), f64(b2), f64(gamma), f64(beta)
    b, n_anchors = tri.shape
    n_comp, apc, _ = W1.shape
    d = W2.shape[2]
    x = np.transpose(tri.reshape(b, apc, n_comp), (2, 0, 1))
    h = (mxq(x, 2, "e4m3") @ mxq(W1, 1, "e4m3")) + b1[:, None, :]
    h = np.square(np.maximum(h, 0.0))
    y = (mxq(h, 2, "e4m3") @ mxq(W2, 1, "e4m3")) + b2[:, None, :]
    mu = np.mean(y, axis=-1, keepdims=True)
    var = np.mean(np.square(y - mu), axis=-1, keepdims=True)
    y = (y - mu) * (1.0 / np.sqrt(var + LN_EPS))
    y = y * gamma[:, None, :] + beta[:, None, :]
    return np.transpose(y, (1, 0, 2)).reshape(b, n_comp * d)

@@ -1,0 +1,424 @@
+from contextlib import ExitStack
+
+import concourse.mybir as mybir
+from concourse.masks import make_identity
+
+F32 = mybir.dt.float32
+BF16 = mybir.dt.bfloat16
+U32 = mybir.dt.uint32
+U8 = mybir.dt.uint8
+FP8X4 = mybir.dt.float8_e4m3fn_x4
+ACT = mybir.ActivationFunctionType
+ALU = mybir.AluOpType
+
+P = 128
+B, K1, H, D = 4096, 512, 1024, 512
+CH = 512
+NCH = B // CH
+BT = CH // P
+LN_EPS = 1e-5
+GCOLS = 128
+
+FLOPS = 2 * B * K1 * H + 2 * B * H * D
+
+
+def tile_patchwork_t_kernel(tc, tri, W1, b1, W2, b2, gamma, beta, out):
+    nc = tc.nc
+    with ExitStack() as ctx:
+        keep = ctx.enter_context(tc.tile_pool(name="keep", bufs=1))
+        tgpool = ctx.enter_context(tc.tile_pool(name="tgpool", bufs=2))
+        tcpool = ctx.enter_context(tc.tile_pool(name="tcpool", bufs=3))
+        rpool = ctx.enter_context(tc.tile_pool(name="rpool", bufs=4))
+        hpool0 = ctx.enter_context(tc.tile_pool(name="hpool0", bufs=1))
+        hpool1 = ctx.enter_context(tc.tile_pool(name="hpool1", bufs=2))
+        cpool = ctx.enter_context(tc.tile_pool(name="cpool", bufs=2))
+        ypool = ctx.enter_context(tc.tile_pool(name="ypool", bufs=3))
+        opool = ctx.enter_context(tc.tile_pool(name="opool", bufs=3))
+        spool = ctx.enter_context(tc.tile_pool(name="spool", bufs=3))
+        pgb = ctx.enter_context(tc.psum_pool(name="pgb", bufs=1))
+        ptr = ctx.enter_context(tc.psum_pool(name="ptr", bufs=1))
+        ph = ctx.enter_context(tc.psum_pool(name="ph", bufs=4))
+        py = ctx.enter_context(tc.psum_pool(name="py", bufs=2))
+        banks = {"tr": ptr, "h": ph, "y": py}
+
+        traw = keep.tile([P, NCH * BT * K1], BF16, name="traw")
+        w1raw = keep.tile([P, 4, H], BF16, name="w1raw")
+        w2raw = keep.tile([P, 2, 4, D], BF16, name="w2raw")
+        b1raw = keep.tile([P, 2, 4], BF16, name="b1raw")
+        b1f = keep.tile([P, 8], F32, name="b1f")
+        vec = keep.tile([P, 3 * D], BF16, name="vec")
+        ones = keep.tile([P, P], BF16, name="ones")
+        ident = keep.tile([P, P], F32, name="ident")
+        epst = keep.tile([P, 1], F32, name="epst")
+        warm = keep.tile([P, 1], F32, name="warm")
+        b2b = keep.tile([P, D], F32, name="b2b")
+        betf = keep.tile([P, D], F32, name="betf")
+        junk = keep.tile([P, D], BF16, name="junk")
+        w1g = keep.tile([P, 4 * H], BF16, name="w1g", align_bytes=64)
+        w1c = keep.tile([P, H], U32, name="w1c", align_bytes=64)
+        w1s = keep.tile([P, H], U8, name="w1s", align_bytes=64)
+        w2g = keep.tile([P, 2, D, 4], BF16, name="w2g", align_bytes=64)
+        w2c = keep.tile([P, 2 * D], U32, name="w2c", align_bytes=64)
+        w2s = keep.tile([P, 2 * D], U8, name="w2s", align_bytes=64)
+        gb = pgb.tile([P, 2 * D], BF16, name="gb")
+        gam = gb[:, 0:D]
+        bet = gb[:, D:2 * D]
+
+        make_identity(nc, ident[:])
+        ctx.enter_context(tc.manual_schedule())
+
+        w1v = W1.rearrange("o k h -> (o k) h")
+        w2v = W2.rearrange("o k d -> (o k) d")
+        live = {}
+
+        def ok(c):
+            return 0 <= c < NCH
+
+        def copy_on(eng, dst, src):
+            if eng == "V":
+                nc.vector.tensor_copy(out=dst, in_=src)
+            else:
+                nc.scalar.copy(out=dst, in_=src)
+
+        def ld_tri(c):
+            nc.sync.dma_start(
+                out=traw[:, c * BT * K1:(c + 1) * BT * K1],
+                in_=tri[c * CH:(c + 1) * CH, :].rearrange("(p t) k -> p (t k)", t=BT),
+            )
+
+        def ld_w1(g):
+            nc.sync.dma_start(
+                out=w1raw[:, :, g * 512:(g + 1) * 512],
+                in_=w1v[:, g * 512:(g + 1) * 512].rearrange("(q e) h -> q e h", e=4),
+            )
+
+        def rw1(g, eng):
+            copy_on(
+                eng,
+                w1g[:, g * 2048:(g + 1) * 2048].rearrange("p (t q j) -> p t q j", t=4, q=P, j=4),
+                w1raw[:, :, g * 512:(g + 1) * 512].rearrange("p j (q t) -> p t q j", t=4),
+            )
+
+        def qw1(g):
+            nc.vector.quantize_mx(
+                out=w1c[:, g * 512:(g + 1) * 512].bitcast(FP8X4),
+                scales=w1s[:, g * 512:(g + 1) * 512],
+                in_=w1g[:, g * 2048:(g + 1) * 2048],
+            )
+
+        def rw2(g):
+            nc.vector.tensor_copy(out=w2g[:, g, :, :], in_=w2raw[:, g, :, :].rearrange("p t d -> p d t"))
+
+        def qw2():
+            nc.vector.quantize_mx(
+                out=w2c[:].bitcast(FP8X4), scales=w2s[:], in_=w2g[:].rearrange("p g d t -> p (g d t)"),
+            )
+
+        def spread():
+            pbt = py.tile([P, D], F32, name="pbt", tag="y")
+            nc.tensor.matmul(out=pbt[:], lhsT=ones[:], rhs=vec[:, 0:D], start=True, stop=True)
+            nc.tensor.matmul(out=gam, lhsT=ones[:], rhs=vec[:, D:2 * D], start=True, stop=True)
+            nc.tensor.matmul(out=bet, lhsT=ones[:], rhs=vec[:, 2 * D:3 * D], start=True, stop=True)
+            live["pb"] = pbt
+
+        def op_t(c, hf, bank="tr"):
+            if not ok(c):
+                return
+            words = traw[:, c * BT * K1:(c + 1) * BT * K1].bitcast(F32)
+            trp = banks[bank].tile([P, 2, 256], F32, name="trp", tag=bank)
+            live["trp", c, hf] = trp
+            for j in range(2):
+                t = 2 * hf + j
+                for u in range(2):
+                    nc.tensor.transpose(
+                        trp[:, u, j * P:(j + 1) * P],
+                        words[:, t * 256 + u:(t + 1) * 256:2],
+                        ident[:],
+                    )
+
+        def op_a(c, hf, eng):
+            if not ok(c):
+                return
+            if hf == 0:
+                live["tg", c] = tgpool.tile([P, 2 * CH], F32, name="tg", tag="tg", align_bytes=64)
+            dst = live["tg", c][:, hf * 512:(hf + 1) * 512].rearrange("p (w u) -> p w u", u=2)
+            copy_on(eng, dst, live["trp", c, hf][:].rearrange("p u w -> p w u"))
+
+        def op_qt(c):
+            if not ok(c):
+                return
+            tcod = tcpool.tile([P, CH], U32, name="tcod", tag="tcod", align_bytes=64)
+            tscl = tcpool.tile([P, CH], U8, name="tscl", tag="tscl", align_bytes=64)
+            nc.vector.quantize_mx(out=tcod[:].bitcast(FP8X4), scales=tscl[:], in_=live["tg", c][:].bitcast(BF16))
+            live["tq", c] = (tcod, tscl)
+
+        def op_mm1(c, m):
+            if not ok(c):
+                return
+            tcod, tscl = live["tq", c]
+            hp = ph.tile([P, CH], F32, name="hp", tag="h")
+            live["hp", c, m] = hp
+            nc.tensor.matmul_mx(
+                out=hp[:],
+                lhsT=w1c[:, m * P:(m + 1) * P].bitcast(FP8X4),
+                lhsT_scale=w1s[:, m * P:(m + 1) * P],
+                rhs=tcod[:].bitcast(FP8X4),
+                rhs_scale=tscl[:],
+                start=True,
+                stop=True,
+            )
+
+        def op_h1(c, m):
+            if not ok(c):
+                return
+            g, t = divmod(m, 4)
+            if t == 0:
+                live["r", c, g] = rpool.tile([P, 4, CH], F32, name="r", tag="r")
+            nc.scalar.activation(
+                out=live["r", c, g][:, t, :], in_=live["hp", c, m][:], func=ACT.Relu, bias=b1f[:, m:m + 1], scale=1.0,
+            )
+
+        def op_h2(c, g, w0, w1, eng):
+            if not ok(c):
+                return
+            if ("hb", c, g) not in live:
+                pool = hpool0 if g == 0 else hpool1
+                live["hb", c, g] = pool.tile([P, CH, 4], BF16, name="hb%d" % g, tag="hb%d" % g, align_bytes=64)
+            hb = live["hb", c, g]
+            r = live["r", c, g]
+            if eng == "S":
+                nc.scalar.activation(
+                    out=hb[:, w0:w1, :].rearrange("p (c i) t -> p c t i", i=4),
+                    in_=r[:, :, w0:w1].rearrange("p t (c i) -> p c t i", i=4),
+                    func=ACT.Square,
+                )
+            else:
+                src = r[:, :, w0:w1].rearrange("p t w -> p w t")
+                if eng == "V":
+                    nc.vector.tensor_tensor(out=hb[:, w0:w1, :], in0=src, in1=src, op=ALU.mult)
+                else:
+                    nc.gpsimd.tensor_tensor(out=hb[:, w0:w1, :], in0=src, in1=src, op=ALU.mult)
+
+        def op_qh(c, g):
+            if not ok(c):
+                return
+            hcod = cpool.tile([P, CH], U32, name="hcod%d" % g, tag="hcod%d" % g, align_bytes=64)
+            hscl = cpool.tile([P, CH], U8, name="hscl%d" % g, tag="hscl%d" % g, align_bytes=64)
+            live["hq", c, g] = (hcod, hscl)
+            nc.vector.quantize_mx(
+                out=hcod[:].bitcast(FP8X4), scales=hscl[:], in_=live["hb", c, g][:].rearrange("p w t -> p (w t)"),
+            )
+
+        def op_mm2(c, t, bank="y"):
+            if not ok(c):
+                return
+            yp = banks[bank].tile([P, D], F32, name="yp", tag=bank)
+            live["yp", c, t] = yp
+            for g in range(2):
+                hcod, hscl = live["hq", c, g]
+                nc.tensor.matmul_mx(
+                    out=yp[:],
+                    lhsT=hcod[:, t * P:(t + 1) * P].bitcast(FP8X4),
+                    lhsT_scale=hscl[:, t * P:(t + 1) * P],
+                    rhs=w2c[:, g * D:(g + 1) * D].bitcast(FP8X4),
+                    rhs_scale=w2s[:, g * D:(g + 1) * D],
+                    start=(g == 0),
+                    stop=(g == 1),
+                )
+
+        def stat(name, c):
+            if (name, c) not in live:
+                live[name, c] = spool.tile([P, BT], F32, name=name, tag=name)
+            return live[name, c]
+
+        def op_l1(c, t):
+            if not ok(c):
+                return
+            if t == 0:
+                live["y", c] = ypool.tile([P, BT, D], F32, name="y", tag="y")
+            nc.vector.scalar_tensor_tensor(
+                out=live["y", c][:, t, :], in0=live["yp", c, t][:], scalar=0.0, in1=b2b[:],
+                op0=ALU.add, op1=ALU.add, accum_out=stat("sums", c)[:, t:t + 1],
+            )
+
+        def op_nm(c, t0):
+            if not ok(c):
+                return
+            nc.scalar.activation(
+                out=stat("negmu", c)[:, t0:t0 + 2], in_=stat("sums", c)[:, t0:t0 + 2], func=ACT.Copy, scale=-1.0 / D,
+            )
+
+        def op_l2(c, t):
+            if not ok(c):
+                return
+            nc.scalar.activation(
+                out=junk[:], in_=live["y", c][:, t, :], func=ACT.Square, bias=stat("sums", c)[:, t:t + 1], scale=-float(D),
+                accum_out=stat("ssq", c)[:, t:t + 1],
+            )
+
+        def op_sq(c):
+            if not ok(c):
+                return
+            nc.scalar.activation(
+                out=stat("std", c)[:], in_=stat("ssq", c)[:], func=ACT.Sqrt, bias=epst[:, 0:1], scale=1.0 / (D * D * D),
+            )
+
+        def op_rc(c):
+            if not ok(c):
+                return
+            nc.vector.reciprocal(out=stat("rstd", c)[:], in_=stat("std", c)[:])
+
+        def op_l3(c, t):
+            if not ok(c):
+                return
+            if ("o", c) not in live:
+                live["o", c] = opool.tile([P, BT, D], F32, name="o", tag="o")
+            nc.vector.scalar_tensor_tensor(
+                out=live["o", c][:, t, :], in0=live["y", c][:, t, :], scalar=stat("negmu", c)[:, t:t + 1], in1=gam,
+                op0=ALU.add, op1=ALU.mult,
+            )
+
+        def op_l4(c, t):
+            if not ok(c):
+                return
+            o = live["o", c]
+            nc.vector.scalar_tensor_tensor(
+                out=o[:, t, :], in0=o[:, t, :], scalar=stat("rstd", c)[:, t:t + 1], in1=bet,
+                op0=ALU.mult, op1=ALU.add,
+            )
+
+        def op_l4_sg(c, t):
+            o = live["o", c]
+            nc.scalar.activation(out=o[:, t, :], in_=o[:, t, :], func=ACT.Copy, scale=stat("rstd", c)[:, t:t + 1])
+            nc.gpsimd.tensor_tensor(out=o[:, t, :], in0=o[:, t, :], in1=betf[:], op=ALU.add)
+
+        def op_st(c, t0, t1):
+            if not ok(c):
+                return
+            nc.sync.dma_start(
+                out=out[c * CH:(c + 1) * CH, :].rearrange("(p t) d -> p t d", t=BT)[:, t0:t1, :],
+                in_=live["o", c][:, t0:t1, :],
+            )
+
+        ld_tri(0)
+        ld_w1(0)
+        ld_w1(1)
+        nc.sync.dma_start(out=w2raw[:], in_=w2v.rearrange("(g p t) d -> p g t d", g=2, t=4))
+        for c in range(1, NCH):
+            ld_tri(c)
+        nc.vector.memset(vec[:], 0.0)
+        nc.scalar.dma_start(out=b1raw[:], in_=b1.rearrange("o (g p t) -> p (o g) t", g=2, t=4))
+        for j, v in enumerate((b2, gamma, beta)):
+            nc.scalar.dma_start(out=vec[0:1, j * D:(j + 1) * D], in_=v)
+        nc.vector.memset(epst[:], LN_EPS)
+        nc.vector.memset(ones[:], 1.0)
+        nc.scalar.activation(out=warm[:], in_=epst[:], func=ACT.Sqrt)
+
+        op_t(0, 0, "h")
+        op_t(0, 1, "h")
+        rw1(0, "V")
+        op_a(0, 0, "S")
+        op_a(0, 1, "S")
+        nc.vector.tensor_copy(out=b1f[:], in_=b1raw[:].rearrange("p g t -> p (g t)"))
+        qw1(0)
+        op_qt(0)
+        for m in range(4):
+            op_mm1(0, m)
+        rw1(1, "S")
+        rw2(0)
+        qw1(1)
+        rw2(1)
+        qw2()
+        op_t(1, 0)
+        op_t(1, 1, "y")
+        spread()
+        for m in range(4):
+            op_h1(0, m)
+            op_mm1(0, 4 + m)
+        op_a(1, 0, "S")
+        op_a(1, 1, "S")
+        op_qt(1)
+        op_t(2, 0)
+        for m in range(4):
+            op_h1(0, 4 + m)
+            op_mm1(1, m)
+        nc.vector.tensor_copy(out=b2b[:], in_=live["pb"][:])
+        op_h2(0, 0, 0, 256, "V")
+        op_a(2, 0, "V")
+        op_t(2, 1)
+        op_h2(0, 0, 256, CH, "V")
+        op_h2(0, 1, 0, 256, "S")
+        op_h2(0, 1, 256, CH, "V")
+        op_h1(1, 0)
+        op_mm1(1, 4)
+        op_a(2, 1, "S")
+        op_t(3, 0)
+
+        for c in range(1, NCH + 1):
+            last = c == NCH
+            op_qt(c + 1)
+            op_rc(c - 2)
+            op_qh(c - 1, 1)
+            op_qh(c - 1, 0)
+            for m in range(1, 4):
+                op_h1(c, m)
+                op_mm1(c, 4 + m)
+            op_h2(c, 0, 0, CH, "G")
+            for j in range(2):
+                op_h1(c, 4 + j)
+                op_mm2(c - 1, j)
+                op_mm1(c + 1, j)
+            if last:
+                op_mm2(c - 1, 2, "h")
+                op_mm2(c - 1, 3, "h")
+            op_a(c + 2, 0, "V")
+            op_l4(c - 2, 0)
+            op_l4(c - 2, 1)
+            op_st(c - 2, 0, 2)
+            if last:
+                nc.scalar.copy(out=betf[:], in_=bet)
+                op_l4_sg(c - 2, 2)
+                op_l4_sg(c - 2, 3)
+                op_st(c - 2, 2, 4)
+            for j in range(2):
+                op_l1(c - 1, j)
+                if not last:
+                    op_mm2(c - 1, 2 + j)
+            for j in range(2):
+                op_h1(c, 6 + j)
+                op_mm1(c + 1, 2 + j)
+            op_h1(c + 1, 0)
+            op_t(c + 2, 1)
+            op_mm1(c + 1, 4)
+            op_h2(c, 1, CH - GCOLS, CH, "G")
+            op_h2(c, 1, 0, CH - GCOLS, "S")
+            if not last:
+                op_l4(c - 2, 2)
+                op_l4(c - 2, 3)
+                op_st(c - 2, 2, 4)
+            op_l1(c - 1, 2)
+            op_l1(c - 1, 3)
+            op_l2(c - 1, 0)
+            op_nm(c - 1, 0)
+            op_l2(c - 1, 1)
+            op_l2(c - 1, 2)
+            op_nm(c - 1, 2)
+            op_l2(c - 1, 3)
+            op_a(c + 2, 1, "S")
+            op_sq(c - 1)
+            op_t(c + 3, 0)
+            if not last:
+                for t in range(BT):
+                    op_l3(c - 1, t)
+
+        e = NCH - 1
+        op_l3(e, 0)
+        op_l3(e, 1)
+        op_l3(e, 3)
+        op_rc(e)
+        op_l3(e, 2)
+        op_l4_sg(e, 3)
+        for t in range(3):
+            op_l4(e, t)
+            op_st(e, t, t + 1)
+        op_st(e, 3, 4)

@@ -53,7 +53,7 @@ def tile_patchwork_t_kernel(tc, tri, W1, b1, W2, b2, gamma, beta, out):
         warm = keep.tile([P, 1], F32, name="warm")
         b2b = keep.tile([P, D], F32, name="b2b")
         betf = keep.tile([P, D], F32, name="betf")
-        junk = keep.tile([P, D], BF16, name="junk")
+        junk = keep.tile([P, BT, D], BF16, name="junk")
         w1g = keep.tile([P, 4 * H], BF16, name="w1g", align_bytes=64)
         w1c = keep.tile([P, H], U32, name="w1c", align_bytes=64)
         w1s = keep.tile([P, H], U8, name="w1s", align_bytes=64)
@@ -252,7 +252,7 @@ def tile_patchwork_t_kernel(tc, tri, W1, b1, W2, b2, gamma, beta, out):
             if not ok(c):
                 return
             nc.scalar.activation(
-                out=junk[:], in_=live["y", c][:, t, :], func=ACT.Square, bias=stat("sums", c)[:, t:t + 1], scale=-float(D),
+                out=junk[:, t, :], in_=live["y", c][:, t, :], func=ACT.Square, bias=stat("sums", c)[:, t:t + 1], scale=-float(D),
                 accum_out=stat("ssq", c)[:, t:t + 1],
             )
 

@@ -17,7 +17,7 @@ CH = 512
 NCH = B // CH
 BT = CH // P
 LN_EPS = 1e-5
-GCOLS = 128
+GCOLS = 256
 
 FLOPS = 2 * B * K1 * H + 2 * B * H * D
 
@@ -357,21 +357,27 @@ def tile_patchwork_t_kernel(tc, tri, W1, b1, W2, b2, gamma, beta, out):
         for c in range(1, NCH + 1):
             last = c == NCH
             op_qt(c + 1)
-            op_rc(c - 2)
             op_qh(c - 1, 1)
+            op_h1(c, 1)
+            op_mm1(c, 5)
+            op_sq(c - 2)
+            op_rc(c - 2)
             op_qh(c - 1, 0)
-            for m in range(1, 4):
+            for m in range(2, 4):
                 op_h1(c, m)
                 op_mm1(c, 4 + m)
             op_h2(c, 0, 0, CH, "G")
-            for j in range(2):
-                op_h1(c, 4 + j)
-                op_mm2(c - 1, j)
-                op_mm1(c + 1, j)
+            op_h1(c, 4)
+            op_mm2(c - 1, 0)
+            op_mm1(c + 1, 0)
+            op_mm2(c - 1, 1)
+            op_a(c + 2, 0, "S")
+            op_t(c + 2, 1)
+            op_h1(c, 5)
+            op_mm1(c + 1, 1)
             if last:
                 op_mm2(c - 1, 2, "h")
                 op_mm2(c - 1, 3, "h")
-            op_a(c + 2, 0, "V")
             op_l4(c - 2, 0)
             op_l4(c - 2, 1)
             op_st(c - 2, 0, 2)
@@ -380,6 +386,8 @@ def tile_patchwork_t_kernel(tc, tri, W1, b1, W2, b2, gamma, beta, out):
                 op_l4_sg(c - 2, 2)
                 op_l4_sg(c - 2, 3)
                 op_st(c - 2, 2, 4)
+            else:
+                op_l4(c - 2, 2)
             for j in range(2):
                 op_l1(c - 1, j)
                 if not last:
@@ -388,30 +396,28 @@ def tile_patchwork_t_kernel(tc, tri, W1, b1, W2, b2, gamma, beta, out):
                 op_h1(c, 6 + j)
                 op_mm1(c + 1, 2 + j)
             op_h1(c + 1, 0)
-            op_t(c + 2, 1)
             op_mm1(c + 1, 4)
             op_h2(c, 1, CH - GCOLS, CH, "G")
             op_h2(c, 1, 0, CH - GCOLS, "S")
             if not last:
-                op_l4(c - 2, 2)
                 op_l4(c - 2, 3)
                 op_st(c - 2, 2, 4)
             op_l1(c - 1, 2)
             op_l1(c - 1, 3)
-            op_l2(c - 1, 0)
             op_nm(c - 1, 0)
+            op_l2(c - 1, 0)
             op_l2(c - 1, 1)
-            op_l2(c - 1, 2)
-            op_nm(c - 1, 2)
-            op_l2(c - 1, 3)
             op_a(c + 2, 1, "S")
-            op_sq(c - 1)
+            op_nm(c - 1, 2)
+            op_l2(c - 1, 2)
+            op_l2(c - 1, 3)
             op_t(c + 3, 0)
             if not last:
                 for t in range(BT):
                     op_l3(c - 1, t)
 
         e = NCH - 1
+        op_sq(e)
         op_l3(e, 0)
         op_l3(e, 1)
         op_l3(e, 3)

@@ -80,10 +80,10 @@ def tile_patchwork_t_kernel(tc, tri, W1, b1, W2, b2, gamma, beta, out):
             else:
                 nc.scalar.copy(out=dst, in_=src)
 
-        def ld_tri(c):
+        def ld_tri(c, t0, t1):
             nc.sync.dma_start(
-                out=traw[:, c * BT * K1:(c + 1) * BT * K1],
-                in_=tri[c * CH:(c + 1) * CH, :].rearrange("(p t) k -> p (t k)", t=BT),
+                out=traw[:, (c * BT + t0) * K1:(c * BT + t1) * K1].rearrange("p (t k) -> p t k", k=K1),
+                in_=tri[c * CH:(c + 1) * CH, :].rearrange("(p t) k -> p t k", t=BT)[:, t0:t1, :],
             )
 
         def ld_w1(g):
@@ -92,18 +92,16 @@ def tile_patchwork_t_kernel(tc, tri, W1, b1, W2, b2, gamma, beta, out):
                 in_=w1v[:, g * 512:(g + 1) * 512].rearrange("(q e) h -> q e h", e=4),
             )
 
-        def rw1(g, eng):
+        def rw1(g, t0, t1, eng):
             copy_on(
                 eng,
-                w1g[:, g * 2048:(g + 1) * 2048].rearrange("p (t q j) -> p t q j", t=4, q=P, j=4),
-                w1raw[:, :, g * 512:(g + 1) * 512].rearrange("p j (q t) -> p t q j", t=4),
+                w1g[:, g * 2048 + t0 * 512:g * 2048 + t1 * 512].rearrange("p (t q j) -> p t q j", t=t1 - t0, q=P, j=4),
+                w1raw[:, :, g * 512:(g + 1) * 512].rearrange("p j (q t) -> p t q j", t=4)[:, t0:t1, :, :],
             )
 
-        def qw1(g):
+        def qw1(m0, m1):
             nc.vector.quantize_mx(
-                out=w1c[:, g * 512:(g + 1) * 512].bitcast(FP8X4),
-                scales=w1s[:, g * 512:(g + 1) * 512],
-                in_=w1g[:, g * 2048:(g + 1) * 2048],
+                out=w1c[:, m0 * P:m1 * P].bitcast(FP8X4), scales=w1s[:, m0 * P:m1 * P], in_=w1g[:, m0 * 512:m1 * 512],
             )
 
         def rw2(g):
@@ -256,17 +254,18 @@ def tile_patchwork_t_kernel(tc, tri, W1, b1, W2, b2, gamma, beta, out):
                 accum_out=stat("ssq", c)[:, t:t + 1],
             )
 
-        def op_sq(c):
+        def op_sq(c, t0, t1):
             if not ok(c):
                 return
             nc.scalar.activation(
-                out=stat("std", c)[:], in_=stat("ssq", c)[:], func=ACT.Sqrt, bias=epst[:, 0:1], scale=1.0 / (D * D * D),
+                out=stat("std", c)[:, t0:t1], in_=stat("ssq", c)[:, t0:t1], func=ACT.Sqrt, bias=epst[:, 0:1],
+                scale=1.0 / (D * D * D),
             )
 
-        def op_rc(c):
+        def op_rc(c, t0, t1):
             if not ok(c):
                 return
-            nc.vector.reciprocal(out=stat("rstd", c)[:], in_=stat("std", c)[:])
+            nc.vector.reciprocal(out=stat("rstd", c)[:, t0:t1], in_=stat("std", c)[:, t0:t1])
 
         def op_l3(c, t):
             if not ok(c):
@@ -300,12 +299,14 @@ def tile_patchwork_t_kernel(tc, tri, W1, b1, W2, b2, gamma, beta, out):
                 in_=live["o", c][:, t0:t1, :],
             )
 
-        ld_tri(0)
+        ld_tri(0, 0, 2)
         ld_w1(0)
+        ld_tri(0, 2, 4)
         ld_w1(1)
-        nc.sync.dma_start(out=w2raw[:], in_=w2v.rearrange("(g p t) d -> p g t d", g=2, t=4))
+        for g in range(2):
+            nc.sync.dma_start(out=w2raw[:, g, :, :], in_=w2v[g * 512:(g + 1) * 512, :].rearrange("(p t) d -> p t d", t=4))
         for c in range(1, NCH):
-            ld_tri(c)
+            ld_tri(c, 0, BT)
         nc.vector.memset(vec[:], 0.0)
         nc.scalar.dma_start(out=b1raw[:], in_=b1.rearrange("o (g p t) -> p (o g) t", g=2, t=4))
         for j, v in enumerate((b2, gamma, beta)):
@@ -316,52 +317,58 @@ def tile_patchwork_t_kernel(tc, tri, W1, b1, W2, b2, gamma, beta, out):
 
         op_t(0, 0, "h")
         op_t(0, 1, "h")
-        rw1(0, "V")
         op_a(0, 0, "S")
+        nc.scalar.copy(out=b1f[:], in_=b1raw[:].rearrange("p g t -> p (g t)"))
+        rw1(0, 0, 2, "V")
+        rw1(0, 2, 4, "V")
         op_a(0, 1, "S")
-        nc.vector.tensor_copy(out=b1f[:], in_=b1raw[:].rearrange("p g t -> p (g t)"))
-        qw1(0)
+        rw1(1, 0, 2, "S")
+        qw1(0, 2)
+        qw1(2, 4)
         op_qt(0)
         for m in range(4):
             op_mm1(0, m)
-        rw1(1, "S")
+        rw1(1, 2, 4, "V")
+        qw1(4, 6)
+        qw1(6, 8)
         rw2(0)
-        qw1(1)
         rw2(1)
-        qw2()
-        op_t(1, 0)
-        op_t(1, 1, "y")
-        spread()
         for m in range(4):
             op_h1(0, m)
             op_mm1(0, 4 + m)
-        op_a(1, 0, "S")
-        op_a(1, 1, "S")
-        op_qt(1)
-        op_t(2, 0)
+        op_t(1, 0)
+        op_t(1, 1, "y")
+        spread()
+        op_h2(0, 0, 0, 256, "V")
+        op_h2(0, 0, 256, CH, "V")
+        qw2()
         for m in range(4):
             op_h1(0, 4 + m)
+        op_a(1, 0, "S")
+        op_a(1, 1, "S")
+        op_h2(0, 1, 0, 256, "S")
+        op_qt(1)
+        op_t(2, 0)
+        op_t(2, 1, "y")
+        op_h2(0, 1, 256, CH, "V")
+        for m in range(4):
             op_mm1(1, m)
         nc.vector.tensor_copy(out=b2b[:], in_=live["pb"][:])
-        op_h2(0, 0, 0, 256, "V")
-        op_a(2, 0, "V")
-        op_t(2, 1)
-        op_h2(0, 0, 256, CH, "V")
-        op_h2(0, 1, 0, 256, "S")
-        op_h2(0, 1, 256, CH, "V")
+        op_a(2, 0, "S")
+        op_a(2, 1, "S")
         op_h1(1, 0)
         op_mm1(1, 4)
-        op_a(2, 1, "S")
         op_t(3, 0)
 
-        for c in range(1, NCH + 1):
-            last = c == NCH
+        for c in range(1, NCH):
+            last = c == NCH - 1
+            gcols = 0 if last else GCOLS
             op_qt(c + 1)
             op_qh(c - 1, 1)
             op_h1(c, 1)
             op_mm1(c, 5)
-            op_sq(c - 2)
-            op_rc(c - 2)
+            op_sq(c - 2, 0, BT)
+            op_rc(c - 2, 0, BT)
             op_qh(c - 1, 0)
             for m in range(2, 4):
                 op_h1(c, m)
@@ -375,33 +382,23 @@ def tile_patchwork_t_kernel(tc, tri, W1, b1, W2, b2, gamma, beta, out):
             op_t(c + 2, 1)
             op_h1(c, 5)
             op_mm1(c + 1, 1)
-            if last:
-                op_mm2(c - 1, 2, "h")
-                op_mm2(c - 1, 3, "h")
             op_l4(c - 2, 0)
             op_l4(c - 2, 1)
             op_st(c - 2, 0, 2)
-            if last:
-                nc.scalar.copy(out=betf[:], in_=bet)
-                op_l4_sg(c - 2, 2)
-                op_l4_sg(c - 2, 3)
-                op_st(c - 2, 2, 4)
-            else:
-                op_l4(c - 2, 2)
+            op_l4(c - 2, 2)
             for j in range(2):
                 op_l1(c - 1, j)
-                if not last:
-                    op_mm2(c - 1, 2 + j)
+                op_mm2(c - 1, 2 + j)
             for j in range(2):
                 op_h1(c, 6 + j)
                 op_mm1(c + 1, 2 + j)
             op_h1(c + 1, 0)
             op_mm1(c + 1, 4)
-            op_h2(c, 1, CH - GCOLS, CH, "G")
-            op_h2(c, 1, 0, CH - GCOLS, "S")
-            if not last:
-                op_l4(c - 2, 3)
-                op_st(c - 2, 2, 4)
+            if gcols > 0:
+                op_h2(c, 1, CH - gcols, CH, "G")
+            op_h2(c, 1, 0, CH - gcols, "S")
+            op_l4(c - 2, 3)
+            op_st(c - 2, 2, 4)
             op_l1(c - 1, 2)
             op_l1(c - 1, 3)
             op_nm(c - 1, 0)
@@ -412,19 +409,42 @@ def tile_patchwork_t_kernel(tc, tri, W1, b1, W2, b2, gamma, beta, out):
             op_l2(c - 1, 2)
             op_l2(c - 1, 3)
             op_t(c + 3, 0)
-            if not last:
-                for t in range(BT):
-                    op_l3(c - 1, t)
+            for t in range(2 if last else BT):
+                op_l3(c - 1, t)
 
         e = NCH - 1
-        op_sq(e)
+        op_qh(e, 1)
+        op_qh(e, 0)
+        for t in range(BT):
+            op_mm2(e, t, "y" if t < 2 else "h")
+        nc.scalar.copy(out=betf[:], in_=bet)
+        op_sq(e - 1, 0, BT)
+        op_l3(e - 1, 2)
+        op_rc(e - 1, 0, BT)
+        op_l3(e - 1, 3)
+        for t in range(BT):
+            op_l4_sg(e - 1, t)
+            op_st(e - 1, t, t + 1)
+            op_l1(e, t)
+        op_nm(e, 0)
+        op_l2(e, 0)
+        op_l2(e, 1)
+        op_nm(e, 2)
+        op_l2(e, 2)
+        op_sq(e, 0, 2)
+        op_l2(e, 3)
         op_l3(e, 0)
         op_l3(e, 1)
-        op_l3(e, 3)
-        op_rc(e)
         op_l3(e, 2)
-        op_l4_sg(e, 3)
-        for t in range(3):
-            op_l4(e, t)
-            op_st(e, t, t + 1)
+        op_rc(e, 0, 2)
+        op_sq(e, 2, 4)
+        op_l3(e, 3)
+        op_l4_sg(e, 1)
+        op_l4(e, 0)
+        op_st(e, 0, 1)
+        op_rc(e, 2, 4)
+        op_l4(e, 2)
+        op_st(e, 2, 3)
+        op_l4(e, 3)
+        op_st(e, 1, 2)
         op_st(e, 3, 4)

@@ -17,7 +17,7 @@ CH = 512
 NCH = B // CH
 BT = CH // P
 LN_EPS = 1e-5
-GCOLS = 256
+GCOLS = 192
 
 FLOPS = 2 * B * K1 * H + 2 * B * H * D
 

@@ -378,7 +378,7 @@ def tile_patchwork_t_kernel(tc, tri, W1, b1, W2, b2, gamma, beta, out):
             op_mm2(c - 1, 0)
             op_mm1(c + 1, 0)
             op_mm2(c - 1, 1)
-            op_a(c + 2, 0, "S")
+            op_a(c + 2, 0, "V" if c % 2 == 1 else "S")
             op_t(c + 2, 1)
             op_h1(c, 5)
             op_mm1(c + 1, 1)

@@ -105,7 +105,10 @@ def tile_patchwork_t_kernel(tc, tri, W1, b1, W2, b2, gamma, beta, out):
             )
 
         def rw2(g):
-            nc.vector.tensor_copy(out=w2g[:, g, :, :], in_=w2raw[:, g, :, :].rearrange("p t d -> p d t"))
+            nc.vector.tensor_copy(
+                out=w2g[:, g, :, :].rearrange("p (c i) t -> p c t i", i=4),
+                in_=w2raw[:, g, :, :].rearrange("p t (c i) -> p c t i", i=4),
+            )
 
         def qw2():
             nc.vector.quantize_mx(
@@ -277,12 +280,12 @@ def tile_patchwork_t_kernel(tc, tri, W1, b1, W2, b2, gamma, beta, out):
                 op0=ALU.add, op1=ALU.mult,
             )
 
-        def op_l4(c, t):
+        def op_l4(c, t, d0=0, d1=D):
             if not ok(c):
                 return
             o = live["o", c]
             nc.vector.scalar_tensor_tensor(
-                out=o[:, t, :], in0=o[:, t, :], scalar=stat("rstd", c)[:, t:t + 1], in1=bet,
+                out=o[:, t, d0:d1], in0=o[:, t, d0:d1], scalar=stat("rstd", c)[:, t:t + 1], in1=bet[:, d0:d1],
                 op0=ALU.mult, op1=ALU.add,
             )
 
@@ -291,12 +294,12 @@ def tile_patchwork_t_kernel(tc, tri, W1, b1, W2, b2, gamma, beta, out):
             nc.scalar.activation(out=o[:, t, :], in_=o[:, t, :], func=ACT.Copy, scale=stat("rstd", c)[:, t:t + 1])
             nc.gpsimd.tensor_tensor(out=o[:, t, :], in0=o[:, t, :], in1=betf[:], op=ALU.add)
 
-        def op_st(c, t0, t1):
+        def op_st(c, t0, t1, d0=0, d1=D):
             if not ok(c):
                 return
             nc.sync.dma_start(
-                out=out[c * CH:(c + 1) * CH, :].rearrange("(p t) d -> p t d", t=BT)[:, t0:t1, :],
-                in_=live["o", c][:, t0:t1, :],
+                out=out[c * CH:(c + 1) * CH, :].rearrange("(p t) d -> p t d", t=BT)[:, t0:t1, d0:d1],
+                in_=live["o", c][:, t0:t1, d0:d1],
             )
 
         ld_tri(0, 0, 2)
@@ -362,7 +365,7 @@ def tile_patchwork_t_kernel(tc, tri, W1, b1, W2, b2, gamma, beta, out):
 
         for c in range(1, NCH):
             last = c == NCH - 1
-            gcols = 0 if last else GCOLS
+            gcols = GCOLS // 2 if last else GCOLS
             op_qt(c + 1)
             op_qh(c - 1, 1)
             op_h1(c, 1)
@@ -394,8 +397,7 @@ def tile_patchwork_t_kernel(tc, tri, W1, b1, W2, b2, gamma, beta, out):
                 op_mm1(c + 1, 2 + j)
             op_h1(c + 1, 0)
             op_mm1(c + 1, 4)
-            if gcols > 0:
-                op_h2(c, 1, CH - gcols, CH, "G")
+            op_h2(c, 1, CH - gcols, CH, "G")
             op_h2(c, 1, 0, CH - gcols, "S")
             op_l4(c - 2, 3)
             op_st(c - 2, 2, 4)
@@ -413,8 +415,8 @@ def tile_patchwork_t_kernel(tc, tri, W1, b1, W2, b2, gamma, beta, out):
                 op_l3(c - 1, t)
 
         e = NCH - 1
-        op_qh(e, 1)
         op_qh(e, 0)
+        op_qh(e, 1)
         for t in range(BT):
             op_mm2(e, t, "y" if t < 2 else "h")
         nc.scalar.copy(out=betf[:], in_=bet)
@@ -445,6 +447,7 @@ def tile_patchwork_t_kernel(tc, tri, W1, b1, W2, b2, gamma, beta, out):
         op_rc(e, 2, 4)
         op_l4(e, 2)
         op_st(e, 2, 3)
-        op_l4(e, 3)
         op_st(e, 1, 2)
-        op_st(e, 3, 4)
+        for d0 in range(0, D, D // 2):
+            op_l4(e, 3, d0, d0 + D // 2)
+            op_st(e, 3, 4, d0, d0 + D // 2)

from contextlib import ExitStack

import concourse.mybir as mybir
from concourse.masks import make_identity

F32 = mybir.dt.float32
BF16 = mybir.dt.bfloat16
U32 = mybir.dt.uint32
U8 = mybir.dt.uint8
FP8X4 = mybir.dt.float8_e4m3fn_x4
ACT = mybir.ActivationFunctionType
ALU = mybir.AluOpType

P = 128
B, K1, H, D = 4096, 512, 1024, 512
CH = 512
NCH = B // CH
BT = CH // P
LN_EPS = 1e-5
GCOLS = 192

FLOPS = 2 * B * K1 * H + 2 * B * H * D


def tile_patchwork_t_kernel(tc, tri, W1, b1, W2, b2, gamma, beta, out):
    nc = tc.nc
    with ExitStack() as ctx:
        keep = ctx.enter_context(tc.tile_pool(name="keep", bufs=1))
        tgpool = ctx.enter_context(tc.tile_pool(name="tgpool", bufs=2))
        tcpool = ctx.enter_context(tc.tile_pool(name="tcpool", bufs=3))
        rpool = ctx.enter_context(tc.tile_pool(name="rpool", bufs=4))
        hpool0 = ctx.enter_context(tc.tile_pool(name="hpool0", bufs=1))
        hpool1 = ctx.enter_context(tc.tile_pool(name="hpool1", bufs=2))
        cpool = ctx.enter_context(tc.tile_pool(name="cpool", bufs=2))
        ypool = ctx.enter_context(tc.tile_pool(name="ypool", bufs=3))
        opool = ctx.enter_context(tc.tile_pool(name="opool", bufs=3))
        spool = ctx.enter_context(tc.tile_pool(name="spool", bufs=3))
        pgb = ctx.enter_context(tc.psum_pool(name="pgb", bufs=1))
        ptr = ctx.enter_context(tc.psum_pool(name="ptr", bufs=1))
        ph = ctx.enter_context(tc.psum_pool(name="ph", bufs=4))
        py = ctx.enter_context(tc.psum_pool(name="py", bufs=2))
        banks = {"tr": ptr, "h": ph, "y": py}

        traw = keep.tile([P, NCH * BT * K1], BF16, name="traw")
        w1raw = keep.tile([P, 4, H], BF16, name="w1raw")
        w2raw = keep.tile([P, 2, 4, D], BF16, name="w2raw")
        b1raw = keep.tile([P, 2, 4], BF16, name="b1raw")
        b1f = keep.tile([P, 8], F32, name="b1f")
        vec = keep.tile([P, 3 * D], BF16, name="vec")
        ones = keep.tile([P, P], BF16, name="ones")
        ident = keep.tile([P, P], F32, name="ident")
        epst = keep.tile([P, 1], F32, name="epst")
        warm = keep.tile([P, 1], F32, name="warm")
        b2b = keep.tile([P, D], F32, name="b2b")
        betf = keep.tile([P, D], F32, name="betf")
        junk = keep.tile([P, BT, D], BF16, name="junk")
        w1g = keep.tile([P, 4 * H], BF16, name="w1g", align_bytes=64)
        w1c = keep.tile([P, H], U32, name="w1c", align_bytes=64)
        w1s = keep.tile([P, H], U8, name="w1s", align_bytes=64)
        w2g = keep.tile([P, 2, D, 4], BF16, name="w2g", align_bytes=64)
        w2c = keep.tile([P, 2 * D], U32, name="w2c", align_bytes=64)
        w2s = keep.tile([P, 2 * D], U8, name="w2s", align_bytes=64)
        gb = pgb.tile([P, 2 * D], BF16, name="gb")
        gam = gb[:, 0:D]
        bet = gb[:, D:2 * D]

        make_identity(nc, ident[:])
        ctx.enter_context(tc.manual_schedule())

        w1v = W1.rearrange("o k h -> (o k) h")
        w2v = W2.rearrange("o k d -> (o k) d")
        live = {}

        def ok(c):
            return 0 <= c < NCH

        def copy_on(eng, dst, src):
            if eng == "V":
                nc.vector.tensor_copy(out=dst, in_=src)
            else:
                nc.scalar.copy(out=dst, in_=src)

        def ld_tri(c, t0, t1):
            nc.sync.dma_start(
                out=traw[:, (c * BT + t0) * K1:(c * BT + t1) * K1].rearrange("p (t k) -> p t k", k=K1),
                in_=tri[c * CH:(c + 1) * CH, :].rearrange("(p t) k -> p t k", t=BT)[:, t0:t1, :],
            )

        def ld_w1(g):
            nc.sync.dma_start(
                out=w1raw[:, :, g * 512:(g + 1) * 512],
                in_=w1v[:, g * 512:(g + 1) * 512].rearrange("(q e) h -> q e h", e=4),
            )

        def rw1(g, t0, t1, eng):
            copy_on(
                eng,
                w1g[:, g * 2048 + t0 * 512:g * 2048 + t1 * 512].rearrange("p (t q j) -> p t q j", t=t1 - t0, q=P, j=4),
                w1raw[:, :, g * 512:(g + 1) * 512].rearrange("p j (q t) -> p t q j", t=4)[:, t0:t1, :, :],
            )

        def qw1(m0, m1):
            nc.vector.quantize_mx(
                out=w1c[:, m0 * P:m1 * P].bitcast(FP8X4), scales=w1s[:, m0 * P:m1 * P], in_=w1g[:, m0 * 512:m1 * 512],
            )

        def rw2(g):
            nc.vector.tensor_copy(
                out=w2g[:, g, :, :].rearrange("p (c i) t -> p c t i", i=4),
                in_=w2raw[:, g, :, :].rearrange("p t (c i) -> p c t i", i=4),
            )

        def qw2():
            nc.vector.quantize_mx(
                out=w2c[:].bitcast(FP8X4), scales=w2s[:], in_=w2g[:].rearrange("p g d t -> p (g d t)"),
            )

        def spread():
            pbt = py.tile([P, D], F32, name="pbt", tag="y")
            nc.tensor.matmul(out=pbt[:], lhsT=ones[:], rhs=vec[:, 0:D], start=True, stop=True)
            nc.tensor.matmul(out=gam, lhsT=ones[:], rhs=vec[:, D:2 * D], start=True, stop=True)
            nc.tensor.matmul(out=bet, lhsT=ones[:], rhs=vec[:, 2 * D:3 * D], start=True, stop=True)
            live["pb"] = pbt

        def op_t(c, hf, bank="tr"):
            if not ok(c):
                return
            words = traw[:, c * BT * K1:(c + 1) * BT * K1].bitcast(F32)
            trp = banks[bank].tile([P, 2, 256], F32, name="trp", tag=bank)
            live["trp", c, hf] = trp
            for j in range(2):
                t = 2 * hf + j
                for u in range(2):
                    nc.tensor.transpose(
                        trp[:, u, j * P:(j + 1) * P],
                        words[:, t * 256 + u:(t + 1) * 256:2],
                        ident[:],
                    )

        def op_a(c, hf, eng):
            if not ok(c):
                return
            if hf == 0:
                live["tg", c] = tgpool.tile([P, 2 * CH], F32, name="tg", tag="tg", align_bytes=64)
            dst = live["tg", c][:, hf * 512:(hf + 1) * 512].rearrange("p (w u) -> p w u", u=2)
            copy_on(eng, dst, live["trp", c, hf][:].rearrange("p u w -> p w u"))

        def op_qt(c):
            if not ok(c):
                return
            tcod = tcpool.tile([P, CH], U32, name="tcod", tag="tcod", align_bytes=64)
            tscl = tcpool.tile([P, CH], U8, name="tscl", tag="tscl", align_bytes=64)
            nc.vector.quantize_mx(out=tcod[:].bitcast(FP8X4), scales=tscl[:], in_=live["tg", c][:].bitcast(BF16))
            live["tq", c] = (tcod, tscl)

        def op_mm1(c, m):
            if not ok(c):
                return
            tcod, tscl = live["tq", c]
            hp = ph.tile([P, CH], F32, name="hp", tag="h")
            live["hp", c, m] = hp
            nc.tensor.matmul_mx(
                out=hp[:],
                lhsT=w1c[:, m * P:(m + 1) * P].bitcast(FP8X4),
                lhsT_scale=w1s[:, m * P:(m + 1) * P],
                rhs=tcod[:].bitcast(FP8X4),
                rhs_scale=tscl[:],
                start=True,
                stop=True,
            )

        def op_h1(c, m):
            if not ok(c):
                return
            g, t = divmod(m, 4)
            if t == 0:
                live["r", c, g] = rpool.tile([P, 4, CH], F32, name="r", tag="r")
            nc.scalar.activation(
                out=live["r", c, g][:, t, :], in_=live["hp", c, m][:], func=ACT.Relu, bias=b1f[:, m:m + 1], scale=1.0,
            )

        def op_h2(c, g, w0, w1, eng):
            if not ok(c):
                return
            if ("hb", c, g) not in live:
                pool = hpool0 if g == 0 else hpool1
                live["hb", c, g] = pool.tile([P, CH, 4], BF16, name="hb%d" % g, tag="hb%d" % g, align_bytes=64)
            hb = live["hb", c, g]
            r = live["r", c, g]
            if eng == "S":
                nc.scalar.activation(
                    out=hb[:, w0:w1, :].rearrange("p (c i) t -> p c t i", i=4),
                    in_=r[:, :, w0:w1].rearrange("p t (c i) -> p c t i", i=4),
                    func=ACT.Square,
                )
            else:
                src = r[:, :, w0:w1].rearrange("p t w -> p w t")
                if eng == "V":
                    nc.vector.tensor_tensor(out=hb[:, w0:w1, :], in0=src, in1=src, op=ALU.mult)
                else:
                    nc.gpsimd.tensor_tensor(out=hb[:, w0:w1, :], in0=src, in1=src, op=ALU.mult)

        def op_qh(c, g):
            if not ok(c):
                return
            hcod = cpool.tile([P, CH], U32, name="hcod%d" % g, tag="hcod%d" % g, align_bytes=64)
            hscl = cpool.tile([P, CH], U8, name="hscl%d" % g, tag="hscl%d" % g, align_bytes=64)
            live["hq", c, g] = (hcod, hscl)
            nc.vector.quantize_mx(
                out=hcod[:].bitcast(FP8X4), scales=hscl[:], in_=live["hb", c, g][:].rearrange("p w t -> p (w t)"),
            )

        def op_mm2(c, t, bank="y"):
            if not ok(c):
                return
            yp = banks[bank].tile([P, D], F32, name="yp", tag=bank)
            live["yp", c, t] = yp
            for g in range(2):
                hcod, hscl = live["hq", c, g]
                nc.tensor.matmul_mx(
                    out=yp[:],
                    lhsT=hcod[:, t * P:(t + 1) * P].bitcast(FP8X4),
                    lhsT_scale=hscl[:, t * P:(t + 1) * P],
                    rhs=w2c[:, g * D:(g + 1) * D].bitcast(FP8X4),
                    rhs_scale=w2s[:, g * D:(g + 1) * D],
                    start=(g == 0),
                    stop=(g == 1),
                )

        def stat(name, c):
            if (name, c) not in live:
                live[name, c] = spool.tile([P, BT], F32, name=name, tag=name)
            return live[name, c]

        def op_l1(c, t):
            if not ok(c):
                return
            if t == 0:
                live["y", c] = ypool.tile([P, BT, D], F32, name="y", tag="y")
            nc.vector.scalar_tensor_tensor(
                out=live["y", c][:, t, :], in0=live["yp", c, t][:], scalar=0.0, in1=b2b[:],
                op0=ALU.add, op1=ALU.add, accum_out=stat("sums", c)[:, t:t + 1],
            )

        def op_nm(c, t0):
            if not ok(c):
                return
            nc.scalar.activation(
                out=stat("negmu", c)[:, t0:t0 + 2], in_=stat("sums", c)[:, t0:t0 + 2], func=ACT.Copy, scale=-1.0 / D,
            )

        def op_l2(c, t):
            if not ok(c):
                return
            nc.scalar.activation(
                out=junk[:, t, :], in_=live["y", c][:, t, :], func=ACT.Square, bias=stat("sums", c)[:, t:t + 1], scale=-float(D),
                accum_out=stat("ssq", c)[:, t:t + 1],
            )

        def op_sq(c, t0, t1):
            if not ok(c):
                return
            nc.scalar.activation(
                out=stat("std", c)[:, t0:t1], in_=stat("ssq", c)[:, t0:t1], func=ACT.Sqrt, bias=epst[:, 0:1],
                scale=1.0 / (D * D * D),
            )

        def op_rc(c, t0, t1):
            if not ok(c):
                return
            nc.vector.reciprocal(out=stat("rstd", c)[:, t0:t1], in_=stat("std", c)[:, t0:t1])

        def op_l3(c, t):
            if not ok(c):
                return
            if ("o", c) not in live:
                live["o", c] = opool.tile([P, BT, D], F32, name="o", tag="o")
            nc.vector.scalar_tensor_tensor(
                out=live["o", c][:, t, :], in0=live["y", c][:, t, :], scalar=stat("negmu", c)[:, t:t + 1], in1=gam,
                op0=ALU.add, op1=ALU.mult,
            )

        def op_l4(c, t, d0=0, d1=D):
            if not ok(c):
                return
            o = live["o", c]
            nc.vector.scalar_tensor_tensor(
                out=o[:, t, d0:d1], in0=o[:, t, d0:d1], scalar=stat("rstd", c)[:, t:t + 1], in1=bet[:, d0:d1],
                op0=ALU.mult, op1=ALU.add,
            )

        def op_l4_sg(c, t):
            o = live["o", c]
            nc.scalar.activation(out=o[:, t, :], in_=o[:, t, :], func=ACT.Copy, scale=stat("rstd", c)[:, t:t + 1])
            nc.gpsimd.tensor_tensor(out=o[:, t, :], in0=o[:, t, :], in1=betf[:], op=ALU.add)

        def op_st(c, t0, t1, d0=0, d1=D):
            if not ok(c):
                return
            nc.sync.dma_start(
                out=out[c * CH:(c + 1) * CH, :].rearrange("(p t) d -> p t d", t=BT)[:, t0:t1, d0:d1],
                in_=live["o", c][:, t0:t1, d0:d1],
            )

        ld_tri(0, 0, 2)
        ld_w1(0)
        ld_tri(0, 2, 4)
        ld_w1(1)
        for g in range(2):
            nc.sync.dma_start(out=w2raw[:, g, :, :], in_=w2v[g * 512:(g + 1) * 512, :].rearrange("(p t) d -> p t d", t=4))
        for c in range(1, NCH):
            ld_tri(c, 0, BT)
        nc.vector.memset(vec[:], 0.0)
        nc.scalar.dma_start(out=b1raw[:], in_=b1.rearrange("o (g p t) -> p (o g) t", g=2, t=4))
        for j, v in enumerate((b2, gamma, beta)):
            nc.scalar.dma_start(out=vec[0:1, j * D:(j + 1) * D], in_=v)
        nc.vector.memset(epst[:], LN_EPS)
        nc.vector.memset(ones[:], 1.0)
        nc.scalar.activation(out=warm[:], in_=epst[:], func=ACT.Sqrt)

        op_t(0, 0, "h")
        op_t(0, 1, "h")
        op_a(0, 0, "S")
        nc.scalar.copy(out=b1f[:], in_=b1raw[:].rearrange("p g t -> p (g t)"))
        rw1(0, 0, 2, "V")
        rw1(0, 2, 4, "V")
        op_a(0, 1, "S")
        rw1(1, 0, 2, "S")
        qw1(0, 2)
        qw1(2, 4)
        op_qt(0)
        for m in range(4):
            op_mm1(0, m)
        rw1(1, 2, 4, "V")
        qw1(4, 6)
        qw1(6, 8)
        rw2(0)
        rw2(1)
        for m in range(4):
            op_h1(0, m)
            op_mm1(0, 4 + m)
        op_t(1, 0)
        op_t(1, 1, "y")
        spread()
        op_h2(0, 0, 0, 256, "V")
        op_h2(0, 0, 256, CH, "V")
        qw2()
        for m in range(4):
            op_h1(0, 4 + m)
        op_a(1, 0, "S")
        op_a(1, 1, "S")
        op_h2(0, 1, 0, 256, "S")
        op_qt(1)
        op_t(2, 0)
        op_t(2, 1, "y")
        op_h2(0, 1, 256, CH, "V")
        for m in range(4):
            op_mm1(1, m)
        nc.vector.tensor_copy(out=b2b[:], in_=live["pb"][:])
        op_a(2, 0, "S")
        op_a(2, 1, "S")
        op_h1(1, 0)
        op_mm1(1, 4)
        op_t(3, 0)

        for c in range(1, NCH):
            last = c == NCH - 1
            gcols = GCOLS // 2 if last else GCOLS
            op_qt(c + 1)
            op_qh(c - 1, 1)
            op_h1(c, 1)
            op_mm1(c, 5)
            op_sq(c - 2, 0, BT)
            op_rc(c - 2, 0, BT)
            op_qh(c - 1, 0)
            for m in range(2, 4):
                op_h1(c, m)
                op_mm1(c, 4 + m)
            op_h2(c, 0, 0, CH, "G")
            op_h1(c, 4)
            op_mm2(c - 1, 0)
            op_mm1(c + 1, 0)
            op_mm2(c - 1, 1)
            op_a(c + 2, 0, "V" if c % 2 == 1 else "S")
            op_t(c + 2, 1)
            op_h1(c, 5)
            op_mm1(c + 1, 1)
            op_l4(c - 2, 0)
            op_l4(c - 2, 1)
            op_st(c - 2, 0, 2)
            op_l4(c - 2, 2)
            for j in range(2):
                op_l1(c - 1, j)
                op_mm2(c - 1, 2 + j)
            for j in range(2):
                op_h1(c, 6 + j)
                op_mm1(c + 1, 2 + j)
            op_h1(c + 1, 0)
            op_mm1(c + 1, 4)
            op_h2(c, 1, CH - gcols, CH, "G")
            op_h2(c, 1, 0, CH - gcols, "S")
            op_l4(c - 2, 3)
            op_st(c - 2, 2, 4)
            op_l1(c - 1, 2)
            op_l1(c - 1, 3)
            op_nm(c - 1, 0)
            op_l2(c - 1, 0)
            op_l2(c - 1, 1)
            op_a(c + 2, 1, "S")
            op_nm(c - 1, 2)
            op_l2(c - 1, 2)
            op_l2(c - 1, 3)
            op_t(c + 3, 0)
            for t in range(2 if last else BT):
                op_l3(c - 1, t)

        e = NCH - 1
        op_qh(e, 0)
        op_qh(e, 1)
        for t in range(BT):
            op_mm2(e, t, "y" if t < 2 else "h")
        nc.scalar.copy(out=betf[:], in_=bet)
        op_sq(e - 1, 0, BT)
        op_l3(e - 1, 2)
        op_rc(e - 1, 0, BT)
        op_l3(e - 1, 3)
        for t in range(BT):
            op_l4_sg(e - 1, t)
            op_st(e - 1, t, t + 1)
            op_l1(e, t)
        op_nm(e, 0)
        op_l2(e, 0)
        op_l2(e, 1)
        op_nm(e, 2)
        op_l2(e, 2)
        op_sq(e, 0, 2)
        op_l2(e, 3)
        op_l3(e, 0)
        op_l3(e, 1)
        op_l3(e, 2)
        op_rc(e, 0, 2)
        op_sq(e, 2, 4)
        op_l3(e, 3)
        op_l4_sg(e, 1)
        op_l4(e, 0)
        op_st(e, 0, 1)
        op_rc(e, 2, 4)
        op_l4(e, 2)
        op_st(e, 2, 3)
        op_st(e, 1, 2)
        for d0 in range(0, D, D // 2):
            op_l4(e, 3, d0, d0 + D // 2)
            op_st(e, 3, 4, d0, d0 + D // 2)
